import numpy as np
import ml_dtypes


def mxq(x, axis, fmt="e4m3"):
    dtype, down = {"e4m3": (ml_dtypes.float8_e4m3fn, 7), "e5m2": (ml_dtypes.float8_e5m2, 14)}[fmt]
    v = np.moveaxis(np.asarray(x, np.float32).astype(ml_dtypes.bfloat16).astype(np.float64), axis, -1)
    blocks = v.reshape(v.shape[:-1] + (-1, 32))
    amax = np.abs(blocks).max(-1, keepdims=True)
    byte = np.maximum(np.where(amax > 0, np.frexp(amax)[1] - 1 + 127, 0) - down, 1)
    scale = np.exp2(byte - 127.0)
    codes = (blocks / scale).astype(np.float32).astype(dtype).astype(np.float64)
    return np.moveaxis((codes * scale).reshape(v.shape), -1, axis)


WIDE = False


def mx_kscale(k):
    if not WIDE:
        return np.ones(k)
    levels = np.array([10, -10, 5, -5, 0])
    a = np.random.permutation(np.resize(levels, k // 512 * 4)).reshape(k // 512, 4)
    idx = np.arange(k)
    return np.exp2(a[idx // 512, idx % 128 // 32])


BF16 = ml_dtypes.bfloat16


def bf(x):
    return np.asarray(x, np.float32).astype(BF16)


def f64(x):
    return np.asarray(x).astype(np.float64)


E2M1 = np.array([0.0, 0.5, 1.0, 1.5, 2.0, 3.0, 4.0, 6.0, -0.0, -0.5, -1.0, -1.5, -2.0, -3.0, -4.0, -6.0])


def pack_weight(w, fmt):
    k, n = w.shape
    w = f64(bf(w)).reshape(k // 32, 32, n)
    amax = np.abs(w).max(1)
    if fmt == "e4m3":
        byte = np.frexp(amax)[1] - 1 + 127 - 7
    else:
        mant, ex = np.frexp(amax / 6.0)
        byte = np.where(mant > 0.5, ex, ex - 1) + 127
    byte = np.clip(np.where(amax > 0, byte, 1), 1, 254)
    scaled = (w * np.exp2(127.0 - byte)[:, None, :]).reshape(k, n).astype(np.float32)
    by_word = np.ascontiguousarray(scaled.reshape(k // 512, 128, 4, n).transpose(0, 1, 3, 2))
    if fmt == "e4m3":
        words = by_word.astype(ml_dtypes.float8_e4m3fn).view(np.uint8)
    else:
        c = by_word.astype(ml_dtypes.float4_e2m1fn).view(np.uint8) & 0xF
        words = c[..., 0::2] | (c[..., 1::2] << 4)
    return np.ascontiguousarray(words), np.ascontiguousarray(byte.astype(np.uint8).reshape(k // 512, 16, n))


def unpack_weight(words, scales, fmt):
    g, p, n, _ = words.shape
    if fmt == "e4m3":
        vals = np.ascontiguousarray(words).view(ml_dtypes.float8_e4m3fn).astype(np.float64)
    else:
        nib = np.empty((g, p, n, 4), np.uint8)
        nib[..., 0::2] = words & 0xF
        nib[..., 1::2] = words >> 4
        vals = E2M1[nib]
    vals = vals * np.repeat(np.exp2(scales.astype(np.float64) - 127.0), 8, axis=1)[..., None]
    return vals.transpose(0, 1, 3, 2).reshape(g * 512, n)


B, N, NIN, CTX, H, NOUT = 2, 64, 8192, 3, 1024, 2
F = NIN * CTX


def shift_down(y, d):
    return np.pad(y[:, :-d, :], ((0, 0), (d, 0), (0, 0)))


def shift_up(y, d):
    return np.pad(y[:, d:, :], ((0, 0), (0, d), (0, 0)))


def context_linear(xq, wt, shifts):
    y = xq @ wt[:NIN]
    c = 1
    for d in range(1, CTX // 2 + 1):
        for shift in shifts:
            y = y + shift(xq @ wt[c * NIN:(c + 1) * NIN], d)
            c += 1
    return y


def setup_inputs():
    s, u = mx_kscale(NIN), mx_kscale(H)
    x_l = bf(np.random.standard_normal((B, N, NIN)) * s)
    w_l = np.random.standard_normal((H, F)) / np.sqrt(F) / np.tile(s, CTX) * u[:, None]
    words, scales = pack_weight(np.ascontiguousarray(w_l.T), "e4m3")
    b_l = bf(np.random.standard_normal(H) * 0.3 * u)
    W_bil = bf(np.random.standard_normal((NOUT, H, H)) * 0.2 / np.sqrt(H) / u[None, :, None])
    return {"x_l": x_l, "W_l_words": words, "W_l_scales": scales, "b_l": b_l, "W_bil": W_bil}


def reference(x_l, W_l_words, W_l_scales, b_l, W_bil):
    xq = mxq(f64(x_l), 2, "e4m3")
    hl = np.maximum(context_linear(xq, unpack_weight(W_l_words, W_l_scales, "e4m3"), (shift_down, shift_up)) + f64(b_l), 0.0)
    wb = f64(W_bil).transpose(1, 0, 2).reshape(H, NOUT * H)
    t = mxq(hl, 2, "e4m3") @ mxq(wb, 0, "e4m3")
    return t.reshape(B, N, NOUT, H)

@@ -1,0 +1,244 @@
+from contextlib import ExitStack
+
+import concourse.mybir as mybir
+from concourse.masks import make_identity
+
+F32 = mybir.dt.float32
+BF16 = mybir.dt.bfloat16
+I32 = mybir.dt.int32
+U32 = mybir.dt.uint32
+U8 = mybir.dt.uint8
+FP8X4 = mybir.dt.float8_e4m3fn_x4
+RELU = mybir.ActivationFunctionType.Relu
+ADD = mybir.AluOpType.add
+MAX = mybir.AluOpType.max
+
+P = 128
+PACK = 4
+K_PASS = P * PACK
+SEQS = 2
+SEQ_LEN = 64
+TOKENS = SEQS * SEQ_LEN
+NIN = 8192
+CTX = 3
+H = 1024
+NOUT = 2
+OUT_COLS = NOUT * H
+
+X_GROUPS = NIN // K_PASS
+W_GROUPS = CTX * X_GROUPS
+H_TILES = H // P
+H_PASSES = H // K_PASS
+BANK_COLS = 512
+PSUM_BANKS = 8
+OUT_TILES = OUT_COLS // BANK_COLS
+
+X_QUARTER = 4
+GROUPS_PER_BANK = 2
+W_CHUNK = 2
+W_CHUNKS = W_GROUPS // W_CHUNK
+W_BUFS = 5
+PLANES_PER_TILE = 4
+PLANE_SETS = W_GROUPS // PLANES_PER_TILE
+
+HERE, BEFORE, AFTER = 0, 1, 2
+
+FLOPS = 2 * TOKENS * (CTX * NIN * H + H * OUT_COLS)
+
+
+def tile_bilinearpairedlayer_pa_k_kernel(tc, x_l, W_l_words, W_l_scales, b_l, W_bil, out):
+    nc = tc.nc
+    x_rows = x_l.flatten_outer_dims()
+    out_rows = out.rearrange("b i k g -> (b i) (k g)")
+    w_rows = W_l_words.rearrange("g p n t -> p g (n t)").bitcast(I32)
+    scale_rows = W_l_scales.rearrange("(m a) (quad r) n -> quad r a m n", a=PLANES_PER_TILE, r=4)
+
+    with ExitStack() as stack:
+        keep = stack.enter_context(tc.tile_pool(name="keep", bufs=1))
+        w_ring = stack.enter_context(tc.tile_pool(name="w_ring", bufs=W_BUFS))
+        wb_raw_pool = stack.enter_context(tc.tile_pool(name="wb_raw", bufs=NOUT * H_PASSES))
+        wb_grouped_pool = stack.enter_context(tc.tile_pool(name="wb_grouped", bufs=2))
+        psum = stack.enter_context(tc.psum_pool(name="psum", bufs=PSUM_BANKS))
+        stack.enter_context(tc.manual_schedule())
+
+        ident = keep.tile([P, P], F32)
+        zeros = keep.tile([P, X_GROUPS, SEQS, PACK], BF16)
+        bias_rows = keep.tile([P, P], BF16)
+        bias_rows_f32 = keep.tile([P, P], F32)
+        bias = keep.tile([P, H_TILES], F32)
+        x_raw = keep.tile([P, NIN], BF16)
+        x_here = keep.tile([P, X_GROUPS, TOKENS, PACK], BF16, align_bytes=64)
+        x_before = keep.tile([P, X_GROUPS, TOKENS, PACK], BF16, align_bytes=64)
+        x_after = keep.tile([P, X_GROUPS, TOKENS, PACK], BF16, align_bytes=64)
+        xq_words = keep.tile([P, CTX, X_GROUPS, TOKENS], U32, align_bytes=64)
+        xq_planes = keep.tile([P, CTX, X_GROUPS, TOKENS], U8, align_bytes=64)
+        w_planes = keep.tile([P, PLANE_SETS, H], U8, align_bytes=64)
+        wb_words = keep.tile([P, H_PASSES, OUT_COLS], U32, align_bytes=64)
+        wb_planes = keep.tile([P, H_PASSES, OUT_COLS], U8, align_bytes=64)
+        hl_t = keep.tile([P, H_TILES, TOKENS], BF16)
+        hl_grouped = keep.tile([P, H_PASSES, TOKENS, PACK], BF16, align_bytes=64)
+        hl_words = keep.tile([P, H_PASSES, TOKENS], U32, align_bytes=64)
+        hl_planes = keep.tile([P, H_PASSES, TOKENS], U8, align_bytes=64)
+        out_sb = keep.tile([P, OUT_COLS], F32)
+
+        nc.vector.memset(bias_rows[:], 0.0)
+        nc.vector.memset(w_planes[:].bitcast(I32), 0)
+        nc.vector.memset(zeros[:], 0.0)
+        make_identity(nc, ident[:])
+
+        nc.scalar.dma_start(out=bias_rows[0:H_TILES, :], in_=b_l.rearrange("(j p) -> j p", p=P))
+        for quarter in range(X_GROUPS // X_QUARTER):
+            cols = slice(quarter * X_QUARTER * K_PASS, (quarter + 1) * X_QUARTER * K_PASS)
+            nc.sync.dma_start(out=x_raw[:, cols], in_=x_rows[:, cols])
+
+        for quad in range(4):
+            for r in range(4):
+                first = 32 * quad + r
+                last = first + 4 * (PLANES_PER_TILE - 1)
+                nc.sync.dma_start(
+                    out=w_planes[first : last + 1 : 4, :, :].bitcast(I32),
+                    in_=scale_rows[quad, r].bitcast(I32),
+                )
+
+        wb_raw = {}
+        for k in range(NOUT):
+            for s in range(H_PASSES):
+                raw = wb_raw_pool.tile([P, PACK, H], BF16, name="wb_raw")
+                rows = W_bil[k, s * K_PASS : (s + 1) * K_PASS, :]
+                nc.sync.dma_start(out=raw[:], in_=rows.rearrange("(t p) n -> p t n", p=P))
+                wb_raw[(k, s)] = raw
+
+        def load_w_chunk(i):
+            w = w_ring.tile([P, W_CHUNK, H], U32, align_bytes=64)
+            nc.sync.dma_start(out=w[:].bitcast(I32), in_=w_rows[:, i * W_CHUNK : (i + 1) * W_CHUNK, :])
+            return w
+
+        w_chunks = {}
+        for i in range(W_BUFS):
+            w_chunks[i] = load_w_chunk(i)
+
+        def quantise_x(x_tile, c, quarter):
+            groups = slice(quarter * X_QUARTER, (quarter + 1) * X_QUARTER)
+            nc.vector.quantize_mx(
+                out=xq_words[:, c, groups, :].rearrange("p g w -> p (g w)").bitcast(FP8X4),
+                scales=xq_planes[:, c, groups, :].rearrange("p g w -> p (g w)"),
+                in_=x_tile[:, groups, :, :].rearrange("p g w t -> p (g w t)"),
+            )
+
+        x_pairs = x_raw[:].bitcast(F32)
+        pairs_per_group = K_PASS // 2
+        for quarter in range(X_GROUPS // X_QUARTER):
+            for half in range(X_QUARTER // GROUPS_PER_BANK):
+                g0 = quarter * X_QUARTER + half * GROUPS_PER_BANK
+                xt = psum.tile([P, GROUPS_PER_BANK, 2, TOKENS], F32, tag="bank")
+                for g in range(GROUPS_PER_BANK):
+                    for u in range(2):
+                        first = (g0 + g) * pairs_per_group
+                        nc.tensor.transpose(
+                            xt[:, g, u, :], x_pairs[:, first + u : first + pairs_per_group : 2], ident[:]
+                        )
+                grouped = x_here[:, g0 : g0 + GROUPS_PER_BANK, :, :].bitcast(F32)
+                if half == 0:
+                    nc.scalar.copy(out=grouped, in_=xt[:].rearrange("p g u w -> p g w u"))
+                else:
+                    nc.vector.tensor_copy(out=grouped, in_=xt[:].rearrange("p g u w -> p g w u"))
+            quantise_x(x_here, HERE, quarter)
+
+        nc.vector.tensor_copy(out=bias_rows_f32[:], in_=bias_rows[:])
+        bias_ps = psum.tile([P, P], F32, tag="bank")
+        nc.tensor.transpose(bias_ps[:], bias_rows_f32[:], ident[:])
+        nc.vector.tensor_copy(out=bias[:], in_=bias_ps[:, 0:H_TILES])
+
+        by_seq = "p g (b i) t -> p g b (i t)"
+        here_seq = x_here[:].rearrange(by_seq, b=SEQS)
+        before_seq = x_before[:].rearrange(by_seq, b=SEQS)
+        after_seq = x_after[:].rearrange(by_seq, b=SEQS)
+        kept = (SEQ_LEN - 1) * PACK
+        nc.scalar.copy(out=before_seq[:, :, :, 0:PACK], in_=zeros[:])
+        nc.scalar.copy(out=after_seq[:, :, :, kept:], in_=zeros[:])
+        for quarter in range(X_GROUPS // X_QUARTER):
+            groups = slice(quarter * X_QUARTER, (quarter + 1) * X_QUARTER)
+            nc.scalar.copy(out=before_seq[:, groups, :, PACK:], in_=here_seq[:, groups, :, 0:kept])
+            quantise_x(x_before, BEFORE, quarter)
+        for quarter in range(X_GROUPS // X_QUARTER):
+            groups = slice(quarter * X_QUARTER, (quarter + 1) * X_QUARTER)
+            nc.scalar.copy(out=after_seq[:, groups, :, 0:kept], in_=here_seq[:, groups, :, PACK:])
+            quantise_x(x_after, AFTER, quarter)
+
+        for k in range(NOUT):
+            for s in range(H_PASSES):
+                cols = slice(k * H, (k + 1) * H)
+                wb_grouped = wb_grouped_pool.tile([P, H, PACK], BF16, align_bytes=64)
+                nc.vector.tensor_copy(out=wb_grouped[:], in_=wb_raw[(k, s)][:].rearrange("p t n -> p n t"))
+                nc.vector.quantize_mx(
+                    out=wb_words[:, s, cols].bitcast(FP8X4),
+                    scales=wb_planes[:, s, cols],
+                    in_=wb_grouped[:].rearrange("p n t -> p (n t)"),
+                )
+
+        pre_t = [psum.tile([P, TOKENS], F32, tag="bank", name="pre_t%d" % j) for j in range(H_TILES)]
+        for i in range(W_CHUNKS):
+            w = w_chunks[i]
+            for local in range(W_CHUNK):
+                group = i * W_CHUNK + local
+                c, g = divmod(group, X_GROUPS)
+                plane_set, a = divmod(group, PLANES_PER_TILE)
+                for j in range(H_TILES):
+                    units = slice(j * P, (j + 1) * P)
+                    nc.tensor.matmul_mx(
+                        out=pre_t[j][:],
+                        lhsT=w[:, local, units].bitcast(FP8X4),
+                        lhsT_scale=w_planes[4 * a : P, plane_set, units],
+                        rhs=xq_words[:, c, g, :].bitcast(FP8X4),
+                        rhs_scale=xq_planes[:, c, g, :],
+                        start=(group == 0),
+                        stop=(group == W_GROUPS - 1),
+                    )
+            if i + W_BUFS < W_CHUNKS:
+                w_chunks[i + W_BUFS] = load_w_chunk(i + W_BUFS)
+
+        def hidden_to_words(s):
+            for t in range(PACK):
+                j = s * PACK + t
+                if t % 2 == 0:
+                    nc.scalar.activation(
+                        out=hl_t[:, j, :], in_=pre_t[j][:], func=RELU, bias=bias[:, j : j + 1], scale=1.0
+                    )
+                else:
+                    nc.vector.tensor_scalar(
+                        out=hl_t[:, j, :], in0=pre_t[j][:], scalar1=bias[:, j : j + 1], scalar2=0.0, op0=ADD, op1=MAX
+                    )
+            tiles = slice(s * PACK, (s + 1) * PACK)
+            nc.vector.tensor_copy(out=hl_grouped[:, s, :, :], in_=hl_t[:, tiles, :].rearrange("p t w -> p w t"))
+            nc.vector.quantize_mx(
+                out=hl_words[:, s, :].bitcast(FP8X4),
+                scales=hl_planes[:, s, :],
+                in_=hl_grouped[:, s, :, :].rearrange("p w t -> p (w t)"),
+            )
+
+        def second_layer_passes(s, out_ps):
+            for n in range(OUT_TILES):
+                cols = slice(n * BANK_COLS, (n + 1) * BANK_COLS)
+                nc.tensor.matmul_mx(
+                    out=out_ps[n][:],
+                    lhsT=hl_words[:, s, :].bitcast(FP8X4),
+                    lhsT_scale=hl_planes[:, s, :],
+                    rhs=wb_words[:, s, cols].bitcast(FP8X4),
+                    rhs_scale=wb_planes[:, s, cols],
+                    start=(s == 0),
+                    stop=(s == H_PASSES - 1),
+                )
+
+        hidden_to_words(0)
+        out_ps = [psum.tile([P, BANK_COLS], F32, tag="bank", name="out_ps%d" % n) for n in range(OUT_TILES)]
+        second_layer_passes(0, out_ps)
+        hidden_to_words(1)
+        second_layer_passes(1, out_ps)
+
+        for n in range(OUT_TILES):
+            cols = slice(n * BANK_COLS, (n + 1) * BANK_COLS)
+            if n % 2 == 0:
+                nc.scalar.copy(out=out_sb[:, cols], in_=out_ps[n][:])
+            else:
+                nc.vector.tensor_copy(out=out_sb[:, cols], in_=out_ps[n][:])
+            nc.sync.dma_start(out=out_rows[:, cols], in_=out_sb[:, cols])

@@ -10,6 +10,7 @@ U32 = mybir.dt.uint32
 U8 = mybir.dt.uint8
 FP8X4 = mybir.dt.float8_e4m3fn_x4
 RELU = mybir.ActivationFunctionType.Relu
+COPY = mybir.ActivationFunctionType.Copy
 ADD = mybir.AluOpType.add
 MAX = mybir.AluOpType.max
 
@@ -87,9 +88,7 @@ def tile_bilinearpairedlayer_pa_k_kernel(tc, x_l, W_l_words, W_l_scales, b_l, W_
         make_identity(nc, ident[:])
 
         nc.scalar.dma_start(out=bias_rows[0:H_TILES, :], in_=b_l.rearrange("(j p) -> j p", p=P))
-        for quarter in range(X_GROUPS // X_QUARTER):
-            cols = slice(quarter * X_QUARTER * K_PASS, (quarter + 1) * X_QUARTER * K_PASS)
-            nc.sync.dma_start(out=x_raw[:, cols], in_=x_rows[:, cols])
+        nc.sync.dma_start(out=x_raw[:], in_=x_rows)
 
         for quad in range(4):
             for r in range(4):
@@ -110,7 +109,13 @@ def tile_bilinearpairedlayer_pa_k_kernel(tc, x_l, W_l_words, W_l_scales, b_l, W_
 
         def load_w_chunk(i):
             w = w_ring.tile([P, W_CHUNK, H], U32, align_bytes=64)
-            nc.sync.dma_start(out=w[:].bitcast(I32), in_=w_rows[:, i * W_CHUNK : (i + 1) * W_CHUNK, :])
+            groups = slice(i * W_CHUNK, (i + 1) * W_CHUNK)
+            if i < W_CHUNKS - 1:
+                nc.sync.dma_start(out=w[:].bitcast(I32), in_=w_rows[:, groups, :])
+            else:
+                for s in range(H_PASSES):
+                    units = slice(s * K_PASS, (s + 1) * K_PASS)
+                    nc.sync.dma_start(out=w[:, :, units].bitcast(I32), in_=w_rows[:, groups, units])
             return w
 
         w_chunks = {}
@@ -147,7 +152,7 @@ def tile_bilinearpairedlayer_pa_k_kernel(tc, x_l, W_l_words, W_l_scales, b_l, W_
         nc.vector.tensor_copy(out=bias_rows_f32[:], in_=bias_rows[:])
         bias_ps = psum.tile([P, P], F32, tag="bank")
         nc.tensor.transpose(bias_ps[:], bias_rows_f32[:], ident[:])
-        nc.vector.tensor_copy(out=bias[:], in_=bias_ps[:, 0:H_TILES])
+        nc.scalar.activation(out=bias[:], in_=bias_ps[:, 0:H_TILES], func=COPY)
 
         by_seq = "p g (b i) t -> p g b (i t)"
         here_seq = x_here[:].rearrange(by_seq, b=SEQS)
@@ -179,21 +184,23 @@ def tile_bilinearpairedlayer_pa_k_kernel(tc, x_l, W_l_words, W_l_scales, b_l, W_
         pre_t = [psum.tile([P, TOKENS], F32, tag="bank", name="pre_t%d" % j) for j in range(H_TILES)]
         for i in range(W_CHUNKS):
             w = w_chunks[i]
-            for local in range(W_CHUNK):
-                group = i * W_CHUNK + local
-                c, g = divmod(group, X_GROUPS)
-                plane_set, a = divmod(group, PLANES_PER_TILE)
-                for j in range(H_TILES):
-                    units = slice(j * P, (j + 1) * P)
-                    nc.tensor.matmul_mx(
-                        out=pre_t[j][:],
-                        lhsT=w[:, local, units].bitcast(FP8X4),
-                        lhsT_scale=w_planes[4 * a : P, plane_set, units],
-                        rhs=xq_words[:, c, g, :].bitcast(FP8X4),
-                        rhs_scale=xq_planes[:, c, g, :],
-                        start=(group == 0),
-                        stop=(group == W_GROUPS - 1),
-                    )
+            for s in range(H_PASSES):
+                for local in range(W_CHUNK):
+                    group = i * W_CHUNK + local
+                    c, g = divmod(group, X_GROUPS)
+                    plane_set, a = divmod(group, PLANES_PER_TILE)
+                    for t in range(PACK):
+                        j = s * PACK + t
+                        units = slice(j * P, (j + 1) * P)
+                        nc.tensor.matmul_mx(
+                            out=pre_t[j][:],
+                            lhsT=w[:, local, units].bitcast(FP8X4),
+                            lhsT_scale=w_planes[4 * a : P, plane_set, units],
+                            rhs=xq_words[:, c, g, :].bitcast(FP8X4),
+                            rhs_scale=xq_planes[:, c, g, :],
+                            start=(group == 0),
+                            stop=(group == W_GROUPS - 1),
+                        )
             if i + W_BUFS < W_CHUNKS:
                 w_chunks[i + W_BUFS] = load_w_chunk(i + W_BUFS)
 

@@ -39,8 +39,10 @@ GROUPS_PER_BANK = 2
 W_CHUNK = 2
 W_CHUNKS = W_GROUPS // W_CHUNK
 W_BUFS = 5
-PLANES_PER_TILE = 4
-PLANE_SETS = W_GROUPS // PLANES_PER_TILE
+SCALE_ROWS = K_PASS // 32
+PLANE_STEP = 4
+SCALE_BATCH = 2 * CTX
+SCALE_BATCHES = CTX * SCALE_ROWS // SCALE_BATCH
 
 HERE, BEFORE, AFTER = 0, 1, 2
 
@@ -52,13 +54,13 @@ def tile_bilinearpairedlayer_pa_k_kernel(tc, x_l, W_l_words, W_l_scales, b_l, W_
     x_rows = x_l.flatten_outer_dims()
     out_rows = out.rearrange("b i k g -> (b i) (k g)")
     w_rows = W_l_words.rearrange("g p n t -> p g (n t)").bitcast(I32)
-    scale_rows = W_l_scales.rearrange("(m a) (quad r) n -> quad r a m n", a=PLANES_PER_TILE, r=4)
+    scale_rows = W_l_scales.rearrange("(c g) q n -> c q g n", c=CTX).bitcast(I32)
 
     with ExitStack() as stack:
         keep = stack.enter_context(tc.tile_pool(name="keep", bufs=1))
         w_ring = stack.enter_context(tc.tile_pool(name="w_ring", bufs=W_BUFS))
         wb_raw_pool = stack.enter_context(tc.tile_pool(name="wb_raw", bufs=NOUT * H_PASSES))
-        wb_grouped_pool = stack.enter_context(tc.tile_pool(name="wb_grouped", bufs=2))
+        wb_grouped_pool = stack.enter_context(tc.tile_pool(name="wb_grouped", bufs=1))
         psum = stack.enter_context(tc.psum_pool(name="psum", bufs=PSUM_BANKS))
         stack.enter_context(tc.manual_schedule())
 
@@ -73,7 +75,7 @@ def tile_bilinearpairedlayer_pa_k_kernel(tc, x_l, W_l_words, W_l_scales, b_l, W_
         x_after = keep.tile([P, X_GROUPS, TOKENS, PACK], BF16, align_bytes=64)
         xq_words = keep.tile([P, CTX, X_GROUPS, TOKENS], U32, align_bytes=64)
         xq_planes = keep.tile([P, CTX, X_GROUPS, TOKENS], U8, align_bytes=64)
-        w_planes = keep.tile([P, PLANE_SETS, H], U8, align_bytes=64)
+        w_planes = keep.tile([P, X_GROUPS, H], U8, align_bytes=64)
         wb_words = keep.tile([P, H_PASSES, OUT_COLS], U32, align_bytes=64)
         wb_planes = keep.tile([P, H_PASSES, OUT_COLS], U8, align_bytes=64)
         hl_t = keep.tile([P, H_TILES, TOKENS], BF16)
@@ -88,30 +90,38 @@ def tile_bilinearpairedlayer_pa_k_kernel(tc, x_l, W_l_words, W_l_scales, b_l, W_
         make_identity(nc, ident[:])
 
         nc.scalar.dma_start(out=bias_rows[0:H_TILES, :], in_=b_l.rearrange("(j p) -> j p", p=P))
-        nc.sync.dma_start(out=x_raw[:], in_=x_rows)
 
-        for quad in range(4):
-            for r in range(4):
-                first = 32 * quad + r
-                last = first + 4 * (PLANES_PER_TILE - 1)
-                nc.sync.dma_start(
-                    out=w_planes[first : last + 1 : 4, :, :].bitcast(I32),
-                    in_=scale_rows[quad, r].bitcast(I32),
-                )
+        def load_scale_batch(batch):
+            odd, r = divmod(batch, 4)
+            for upper in range(2):
+                quad = 2 * upper + odd
+                q = 4 * quad + r
+                for c in range(CTX):
+                    row = 32 * quad + PLANE_STEP * c + r
+                    nc.sync.dma_start(
+                        out=w_planes[row : row + 1, :, :].bitcast(I32), in_=scale_rows[c, q : q + 1, :, :]
+                    )
+
+        def large_load(number, out, in_):
+            nc.sync.dma_start(out=out, in_=in_)
+            if number < SCALE_BATCHES:
+                load_scale_batch(number)
+
+        large_load(0, x_raw[:], x_rows)
 
         wb_raw = {}
         for k in range(NOUT):
             for s in range(H_PASSES):
                 raw = wb_raw_pool.tile([P, PACK, H], BF16, name="wb_raw")
                 rows = W_bil[k, s * K_PASS : (s + 1) * K_PASS, :]
-                nc.sync.dma_start(out=raw[:], in_=rows.rearrange("(t p) n -> p t n", p=P))
+                large_load(1 + k * H_PASSES + s, raw[:], rows.rearrange("(t p) n -> p t n", p=P))
                 wb_raw[(k, s)] = raw
 
         def load_w_chunk(i):
             w = w_ring.tile([P, W_CHUNK, H], U32, align_bytes=64)
             groups = slice(i * W_CHUNK, (i + 1) * W_CHUNK)
             if i < W_CHUNKS - 1:
-                nc.sync.dma_start(out=w[:].bitcast(I32), in_=w_rows[:, groups, :])
+                large_load(1 + NOUT * H_PASSES + i, w[:].bitcast(I32), w_rows[:, groups, :])
             else:
                 for s in range(H_PASSES):
                     units = slice(s * K_PASS, (s + 1) * K_PASS)
@@ -188,14 +198,13 @@ def tile_bilinearpairedlayer_pa_k_kernel(tc, x_l, W_l_words, W_l_scales, b_l, W_
                 for local in range(W_CHUNK):
                     group = i * W_CHUNK + local
                     c, g = divmod(group, X_GROUPS)
-                    plane_set, a = divmod(group, PLANES_PER_TILE)
                     for t in range(PACK):
                         j = s * PACK + t
                         units = slice(j * P, (j + 1) * P)
                         nc.tensor.matmul_mx(
                             out=pre_t[j][:],
                             lhsT=w[:, local, units].bitcast(FP8X4),
-                            lhsT_scale=w_planes[4 * a : P, plane_set, units],
+                            lhsT_scale=w_planes[PLANE_STEP * c : P, g, units],
                             rhs=xq_words[:, c, g, :].bitcast(FP8X4),
                             rhs_scale=xq_planes[:, c, g, :],
                             start=(group == 0),

@@ -16,6 +16,7 @@ MAX = mybir.AluOpType.max
 
 P = 128
 PACK = 4
+ALIGN = 256
 K_PASS = P * PACK
 SEQS = 2
 SEQ_LEN = 64
@@ -69,20 +70,20 @@ def tile_bilinearpairedlayer_pa_k_kernel(tc, x_l, W_l_words, W_l_scales, b_l, W_
         bias_rows = keep.tile([P, P], BF16)
         bias_rows_f32 = keep.tile([P, P], F32)
         bias = keep.tile([P, H_TILES], F32)
-        x_raw = keep.tile([P, NIN], BF16)
-        x_here = keep.tile([P, X_GROUPS, TOKENS, PACK], BF16, align_bytes=64)
-        x_before = keep.tile([P, X_GROUPS, TOKENS, PACK], BF16, align_bytes=64)
-        x_after = keep.tile([P, X_GROUPS, TOKENS, PACK], BF16, align_bytes=64)
-        xq_words = keep.tile([P, CTX, X_GROUPS, TOKENS], U32, align_bytes=64)
-        xq_planes = keep.tile([P, CTX, X_GROUPS, TOKENS], U8, align_bytes=64)
-        w_planes = keep.tile([P, X_GROUPS, H], U8, align_bytes=64)
-        wb_words = keep.tile([P, H_PASSES, OUT_COLS], U32, align_bytes=64)
-        wb_planes = keep.tile([P, H_PASSES, OUT_COLS], U8, align_bytes=64)
+        x_raw = keep.tile([P, NIN], BF16, align_bytes=ALIGN)
+        x_here = keep.tile([P, X_GROUPS, TOKENS, PACK], BF16, align_bytes=ALIGN)
+        x_before = keep.tile([P, X_GROUPS, TOKENS, PACK], BF16, align_bytes=ALIGN)
+        x_after = keep.tile([P, X_GROUPS, TOKENS, PACK], BF16, align_bytes=ALIGN)
+        xq_words = keep.tile([P, CTX, X_GROUPS, TOKENS], U32, align_bytes=ALIGN)
+        xq_planes = keep.tile([P, CTX, X_GROUPS, TOKENS], U8, align_bytes=ALIGN)
+        w_planes = keep.tile([P, X_GROUPS, H], U8, align_bytes=ALIGN)
+        wb_words = keep.tile([P, H_PASSES, OUT_COLS], U32, align_bytes=ALIGN)
+        wb_planes = keep.tile([P, H_PASSES, OUT_COLS], U8, align_bytes=ALIGN)
         hl_t = keep.tile([P, H_TILES, TOKENS], BF16)
-        hl_grouped = keep.tile([P, H_PASSES, TOKENS, PACK], BF16, align_bytes=64)
-        hl_words = keep.tile([P, H_PASSES, TOKENS], U32, align_bytes=64)
-        hl_planes = keep.tile([P, H_PASSES, TOKENS], U8, align_bytes=64)
-        out_sb = keep.tile([P, OUT_COLS], F32)
+        hl_grouped = keep.tile([P, H_PASSES, TOKENS, PACK], BF16, align_bytes=ALIGN)
+        hl_words = keep.tile([P, H_PASSES, TOKENS], U32, align_bytes=ALIGN)
+        hl_planes = keep.tile([P, H_PASSES, TOKENS], U8, align_bytes=ALIGN)
+        out_sb = keep.tile([P, OUT_COLS], F32, align_bytes=ALIGN)
 
         nc.vector.memset(bias_rows[:], 0.0)
         nc.vector.memset(w_planes[:].bitcast(I32), 0)
@@ -112,13 +113,13 @@ def tile_bilinearpairedlayer_pa_k_kernel(tc, x_l, W_l_words, W_l_scales, b_l, W_
         wb_raw = {}
         for k in range(NOUT):
             for s in range(H_PASSES):
-                raw = wb_raw_pool.tile([P, PACK, H], BF16, name="wb_raw")
+                raw = wb_raw_pool.tile([P, PACK, H], BF16, name="wb_raw", align_bytes=ALIGN)
                 rows = W_bil[k, s * K_PASS : (s + 1) * K_PASS, :]
                 large_load(1 + k * H_PASSES + s, raw[:], rows.rearrange("(t p) n -> p t n", p=P))
                 wb_raw[(k, s)] = raw
 
         def load_w_chunk(i):
-            w = w_ring.tile([P, W_CHUNK, H], U32, align_bytes=64)
+            w = w_ring.tile([P, W_CHUNK, H], U32, align_bytes=ALIGN)
             groups = slice(i * W_CHUNK, (i + 1) * W_CHUNK)
             if i < W_CHUNKS - 1:
                 large_load(1 + NOUT * H_PASSES + i, w[:].bitcast(I32), w_rows[:, groups, :])
@@ -183,7 +184,7 @@ def tile_bilinearpairedlayer_pa_k_kernel(tc, x_l, W_l_words, W_l_scales, b_l, W_
         for k in range(NOUT):
             for s in range(H_PASSES):
                 cols = slice(k * H, (k + 1) * H)
-                wb_grouped = wb_grouped_pool.tile([P, H, PACK], BF16, align_bytes=64)
+                wb_grouped = wb_grouped_pool.tile([P, H, PACK], BF16, align_bytes=ALIGN)
                 nc.vector.tensor_copy(out=wb_grouped[:], in_=wb_raw[(k, s)][:].rearrange("p t n -> p n t"))
                 nc.vector.quantize_mx(
                     out=wb_words[:, s, cols].bitcast(FP8X4),

@@ -39,6 +39,7 @@ X_QUARTER = 4
 GROUPS_PER_BANK = 2
 W_CHUNK = 2
 W_CHUNKS = W_GROUPS // W_CHUNK
+LAST_PAIR = W_CHUNKS - 2
 W_BUFS = 5
 SCALE_ROWS = K_PASS // 32
 PLANE_STEP = 4
@@ -118,20 +119,26 @@ def tile_bilinearpairedlayer_pa_k_kernel(tc, x_l, W_l_words, W_l_scales, b_l, W_
                 large_load(1 + k * H_PASSES + s, raw[:], rows.rearrange("(t p) n -> p t n", p=P))
                 wb_raw[(k, s)] = raw
 
+        def load_part(i, s, g0, g1):
+            units = slice(s * K_PASS, (s + 1) * K_PASS)
+            groups = slice(i * W_CHUNK + g0, i * W_CHUNK + g1)
+            nc.sync.dma_start(out=w_chunks[i][:, g0:g1, units].bitcast(I32), in_=w_rows[:, groups, units])
+
         def load_w_chunk(i):
-            w = w_ring.tile([P, W_CHUNK, H], U32, align_bytes=ALIGN)
-            groups = slice(i * W_CHUNK, (i + 1) * W_CHUNK)
-            if i < W_CHUNKS - 1:
-                large_load(1 + NOUT * H_PASSES + i, w[:].bitcast(I32), w_rows[:, groups, :])
+            w_chunks[i] = w_ring.tile([P, W_CHUNK, H], U32, align_bytes=ALIGN, name="w")
+            if i < LAST_PAIR:
+                groups = slice(i * W_CHUNK, (i + 1) * W_CHUNK)
+                large_load(1 + NOUT * H_PASSES + i, w_chunks[i][:].bitcast(I32), w_rows[:, groups, :])
             else:
-                for s in range(H_PASSES):
-                    units = slice(s * K_PASS, (s + 1) * K_PASS)
-                    nc.sync.dma_start(out=w[:, :, units].bitcast(I32), in_=w_rows[:, groups, units])
-            return w
+                load_part(i, 0, 0, W_CHUNK)
+            if i == W_CHUNKS - 1:
+                load_part(LAST_PAIR, 1, 0, W_CHUNK)
+                for g in range(W_CHUNK):
+                    load_part(i, 1, g, g + 1)
 
         w_chunks = {}
         for i in range(W_BUFS):
-            w_chunks[i] = load_w_chunk(i)
+            load_w_chunk(i)
 
         def quantise_x(x_tile, c, quarter):
             groups = slice(quarter * X_QUARTER, (quarter + 1) * X_QUARTER)
@@ -193,26 +200,30 @@ def tile_bilinearpairedlayer_pa_k_kernel(tc, x_l, W_l_words, W_l_scales, b_l, W_
                 )
 
         pre_t = [psum.tile([P, TOKENS], F32, tag="bank", name="pre_t%d" % j) for j in range(H_TILES)]
-        for i in range(W_CHUNKS):
-            w = w_chunks[i]
+        def first_layer_passes(i, s):
+            for local in range(W_CHUNK):
+                group = i * W_CHUNK + local
+                c, g = divmod(group, X_GROUPS)
+                for j in range(s * PACK, (s + 1) * PACK):
+                    units = slice(j * P, (j + 1) * P)
+                    nc.tensor.matmul_mx(
+                        out=pre_t[j][:],
+                        lhsT=w_chunks[i][:, local, units].bitcast(FP8X4),
+                        lhsT_scale=w_planes[PLANE_STEP * c : P, g, units],
+                        rhs=xq_words[:, c, g, :].bitcast(FP8X4),
+                        rhs_scale=xq_planes[:, c, g, :],
+                        start=(group == 0),
+                        stop=(group == W_GROUPS - 1),
+                    )
+
+        for i in range(LAST_PAIR):
             for s in range(H_PASSES):
-                for local in range(W_CHUNK):
-                    group = i * W_CHUNK + local
-                    c, g = divmod(group, X_GROUPS)
-                    for t in range(PACK):
-                        j = s * PACK + t
-                        units = slice(j * P, (j + 1) * P)
-                        nc.tensor.matmul_mx(
-                            out=pre_t[j][:],
-                            lhsT=w[:, local, units].bitcast(FP8X4),
-                            lhsT_scale=w_planes[PLANE_STEP * c : P, g, units],
-                            rhs=xq_words[:, c, g, :].bitcast(FP8X4),
-                            rhs_scale=xq_planes[:, c, g, :],
-                            start=(group == 0),
-                            stop=(group == W_GROUPS - 1),
-                        )
+                first_layer_passes(i, s)
             if i + W_BUFS < W_CHUNKS:
-                w_chunks[i + W_BUFS] = load_w_chunk(i + W_BUFS)
+                load_w_chunk(i + W_BUFS)
+        for s in range(H_PASSES):
+            for i in range(LAST_PAIR, W_CHUNKS):
+                first_layer_passes(i, s)
 
         def hidden_to_words(s):
             for t in range(PACK):

@@ -40,11 +40,14 @@ GROUPS_PER_BANK = 2
 W_CHUNK = 2
 W_CHUNKS = W_GROUPS // W_CHUNK
 LAST_PAIR = W_CHUNKS - 2
-W_BUFS = 5
+W_BUFS = 6
 SCALE_ROWS = K_PASS // 32
 PLANE_STEP = 4
 SCALE_BATCH = 2 * CTX
 SCALE_BATCHES = CTX * SCALE_ROWS // SCALE_BATCH
+
+LATE = (NOUT - 1, H_PASSES - 1)
+LATE_COLS = BANK_COLS
 
 HERE, BEFORE, AFTER = 0, 1, 2
 
@@ -111,13 +114,16 @@ def tile_bilinearpairedlayer_pa_k_kernel(tc, x_l, W_l_words, W_l_scales, b_l, W_
 
         large_load(0, x_raw[:], x_rows)
 
+        def wb_rows(k, s):
+            return W_bil[k, s * K_PASS : (s + 1) * K_PASS, :].rearrange("(t p) n -> p t n", p=P)
+
         wb_raw = {}
         for k in range(NOUT):
             for s in range(H_PASSES):
                 raw = wb_raw_pool.tile([P, PACK, H], BF16, name="wb_raw", align_bytes=ALIGN)
-                rows = W_bil[k, s * K_PASS : (s + 1) * K_PASS, :]
-                large_load(1 + k * H_PASSES + s, raw[:], rows.rearrange("(t p) n -> p t n", p=P))
                 wb_raw[(k, s)] = raw
+                if (k, s) != LATE:
+                    large_load(1 + k * H_PASSES + s, raw[:], wb_rows(k, s))
 
         def load_part(i, s, g0, g1):
             units = slice(s * K_PASS, (s + 1) * K_PASS)
@@ -128,17 +134,21 @@ def tile_bilinearpairedlayer_pa_k_kernel(tc, x_l, W_l_words, W_l_scales, b_l, W_
             w_chunks[i] = w_ring.tile([P, W_CHUNK, H], U32, align_bytes=ALIGN, name="w")
             if i < LAST_PAIR:
                 groups = slice(i * W_CHUNK, (i + 1) * W_CHUNK)
-                large_load(1 + NOUT * H_PASSES + i, w_chunks[i][:].bitcast(I32), w_rows[:, groups, :])
+                large_load(NOUT * H_PASSES + i, w_chunks[i][:].bitcast(I32), w_rows[:, groups, :])
             else:
                 load_part(i, 0, 0, W_CHUNK)
             if i == W_CHUNKS - 1:
                 load_part(LAST_PAIR, 1, 0, W_CHUNK)
                 for g in range(W_CHUNK):
                     load_part(i, 1, g, g + 1)
+                late = slice(H - LATE_COLS, H)
+                nc.sync.dma_start(out=wb_raw[LATE][:, :, late], in_=wb_rows(*LATE)[:, :, late])
 
         w_chunks = {}
         for i in range(W_BUFS):
             load_w_chunk(i)
+            if i == 3:
+                nc.sync.dma_start(out=wb_raw[LATE][:, :, 0 : H - LATE_COLS], in_=wb_rows(*LATE)[:, :, 0 : H - LATE_COLS])
 
         def quantise_x(x_tile, c, quarter):
             groups = slice(quarter * X_QUARTER, (quarter + 1) * X_QUARTER)
@@ -188,16 +198,22 @@ def tile_bilinearpairedlayer_pa_k_kernel(tc, x_l, W_l_words, W_l_scales, b_l, W_
             nc.scalar.copy(out=after_seq[:, groups, :, 0:kept], in_=here_seq[:, groups, :, PACK:])
             quantise_x(x_after, AFTER, quarter)
 
+        def quantise_wb(k, s, cols, grouped):
+            out_cols = slice(k * H + cols.start, k * H + cols.stop)
+            nc.vector.quantize_mx(
+                out=wb_words[:, s, out_cols].bitcast(FP8X4),
+                scales=wb_planes[:, s, out_cols],
+                in_=grouped.rearrange("p n t -> p (n t)"),
+            )
+
         for k in range(NOUT):
             for s in range(H_PASSES):
-                cols = slice(k * H, (k + 1) * H)
+                cols = slice(0, H - LATE_COLS if (k, s) == LATE else H)
                 wb_grouped = wb_grouped_pool.tile([P, H, PACK], BF16, align_bytes=ALIGN)
-                nc.vector.tensor_copy(out=wb_grouped[:], in_=wb_raw[(k, s)][:].rearrange("p t n -> p n t"))
-                nc.vector.quantize_mx(
-                    out=wb_words[:, s, cols].bitcast(FP8X4),
-                    scales=wb_planes[:, s, cols],
-                    in_=wb_grouped[:].rearrange("p n t -> p (n t)"),
+                nc.vector.tensor_copy(
+                    out=wb_grouped[:, cols, :], in_=wb_raw[(k, s)][:, :, cols].rearrange("p t n -> p n t")
                 )
+                quantise_wb(k, s, cols, wb_grouped[:, cols, :])
 
         pre_t = [psum.tile([P, TOKENS], F32, tag="bank", name="pre_t%d" % j) for j in range(H_TILES)]
         def first_layer_passes(i, s):
@@ -244,8 +260,8 @@ def tile_bilinearpairedlayer_pa_k_kernel(tc, x_l, W_l_words, W_l_scales, b_l, W_
                 in_=hl_grouped[:, s, :, :].rearrange("p w t -> p (w t)"),
             )
 
-        def second_layer_passes(s, out_ps):
-            for n in range(OUT_TILES):
+        def second_layer_passes(s, banks):
+            for n in banks:
                 cols = slice(n * BANK_COLS, (n + 1) * BANK_COLS)
                 nc.tensor.matmul_mx(
                     out=out_ps[n][:],
@@ -259,14 +275,23 @@ def tile_bilinearpairedlayer_pa_k_kernel(tc, x_l, W_l_words, W_l_scales, b_l, W_
 
         hidden_to_words(0)
         out_ps = [psum.tile([P, BANK_COLS], F32, tag="bank", name="out_ps%d" % n) for n in range(OUT_TILES)]
-        second_layer_passes(0, out_ps)
+        second_layer_passes(0, range(OUT_TILES))
         hidden_to_words(1)
-        second_layer_passes(1, out_ps)
+        second_layer_passes(1, range(OUT_TILES - 1))
+
+        wb_late = wb_grouped_pool.tile([P, H, PACK], BF16, align_bytes=ALIGN, name="wb_grouped")
+        first = H - LATE_COLS
+        split = LATE_COLS // 4
+        late_rows = wb_raw[LATE][:].rearrange("p t n -> p n t")
+        nc.scalar.copy(out=wb_late[:, 0:split, :], in_=late_rows[:, first : first + split, :])
+        nc.vector.tensor_copy(out=wb_late[:, split:LATE_COLS, :], in_=late_rows[:, first + split :, :])
+        quantise_wb(LATE[0], LATE[1], slice(first, H), wb_late[:, 0:LATE_COLS, :])
+        second_layer_passes(1, range(OUT_TILES - 1, OUT_TILES))
 
         for n in range(OUT_TILES):
             cols = slice(n * BANK_COLS, (n + 1) * BANK_COLS)
-            if n % 2 == 0:
-                nc.scalar.copy(out=out_sb[:, cols], in_=out_ps[n][:])
-            else:
+            if n == 2:
                 nc.vector.tensor_copy(out=out_sb[:, cols], in_=out_ps[n][:])
+            else:
+                nc.scalar.copy(out=out_sb[:, cols], in_=out_ps[n][:])
             nc.sync.dma_start(out=out_rows[:, cols], in_=out_sb[:, cols])

@@ -150,6 +150,12 @@ def tile_bilinearpairedlayer_pa_k_kernel(tc, x_l, W_l_words, W_l_scales, b_l, W_
             if i == 3:
                 nc.sync.dma_start(out=wb_raw[LATE][:, :, 0 : H - LATE_COLS], in_=wb_rows(*LATE)[:, :, 0 : H - LATE_COLS])
 
+        def interleave(copy, grouped, rows):
+            copy(
+                out=grouped.rearrange("p (c i) t -> p c t i", i=4),
+                in_=rows.rearrange("p t (c i) -> p c t i", i=4),
+            )
+
         def quantise_x(x_tile, c, quarter):
             groups = slice(quarter * X_QUARTER, (quarter + 1) * X_QUARTER)
             nc.vector.quantize_mx(
@@ -210,9 +216,7 @@ def tile_bilinearpairedlayer_pa_k_kernel(tc, x_l, W_l_words, W_l_scales, b_l, W_
             for s in range(H_PASSES):
                 cols = slice(0, H - LATE_COLS if (k, s) == LATE else H)
                 wb_grouped = wb_grouped_pool.tile([P, H, PACK], BF16, align_bytes=ALIGN)
-                nc.vector.tensor_copy(
-                    out=wb_grouped[:, cols, :], in_=wb_raw[(k, s)][:, :, cols].rearrange("p t n -> p n t")
-                )
+                interleave(nc.vector.tensor_copy, wb_grouped[:, cols, :], wb_raw[(k, s)][:, :, cols])
                 quantise_wb(k, s, cols, wb_grouped[:, cols, :])
 
         pre_t = [psum.tile([P, TOKENS], F32, tag="bank", name="pre_t%d" % j) for j in range(H_TILES)]
@@ -253,45 +257,51 @@ def tile_bilinearpairedlayer_pa_k_kernel(tc, x_l, W_l_words, W_l_scales, b_l, W_
                         out=hl_t[:, j, :], in0=pre_t[j][:], scalar1=bias[:, j : j + 1], scalar2=0.0, op0=ADD, op1=MAX
                     )
             tiles = slice(s * PACK, (s + 1) * PACK)
-            nc.vector.tensor_copy(out=hl_grouped[:, s, :, :], in_=hl_t[:, tiles, :].rearrange("p t w -> p w t"))
+            interleave(nc.vector.tensor_copy, hl_grouped[:, s, :, :], hl_t[:, tiles, :])
             nc.vector.quantize_mx(
                 out=hl_words[:, s, :].bitcast(FP8X4),
                 scales=hl_planes[:, s, :],
                 in_=hl_grouped[:, s, :, :].rearrange("p w t -> p (w t)"),
             )
 
-        def second_layer_passes(s, banks):
-            for n in banks:
-                cols = slice(n * BANK_COLS, (n + 1) * BANK_COLS)
+        cuts = [0, 256, 768, 1280, 1536, 1792, 2048]
+        pieces = [slice(lo, hi) for lo, hi in zip(cuts[:-1], cuts[1:])]
+        late_pieces = (4, 5)
+
+        def second_layer_passes(s, numbers):
+            for n in numbers:
+                if s == 0:
+                    out_ps[n] = psum.tile([P, pieces[n].stop - pieces[n].start], F32, tag="bank", name="out_ps%d" % n)
                 nc.tensor.matmul_mx(
                     out=out_ps[n][:],
                     lhsT=hl_words[:, s, :].bitcast(FP8X4),
                     lhsT_scale=hl_planes[:, s, :],
-                    rhs=wb_words[:, s, cols].bitcast(FP8X4),
-                    rhs_scale=wb_planes[:, s, cols],
+                    rhs=wb_words[:, s, pieces[n]].bitcast(FP8X4),
+                    rhs_scale=wb_planes[:, s, pieces[n]],
                     start=(s == 0),
                     stop=(s == H_PASSES - 1),
                 )
 
+        out_ps = {}
         hidden_to_words(0)
-        out_ps = [psum.tile([P, BANK_COLS], F32, tag="bank", name="out_ps%d" % n) for n in range(OUT_TILES)]
-        second_layer_passes(0, range(OUT_TILES))
+        second_layer_passes(0, range(4))
         hidden_to_words(1)
-        second_layer_passes(1, range(OUT_TILES - 1))
+        second_layer_passes(1, range(4))
+        second_layer_passes(0, late_pieces)
 
         wb_late = wb_grouped_pool.tile([P, H, PACK], BF16, align_bytes=ALIGN, name="wb_grouped")
         first = H - LATE_COLS
         split = LATE_COLS // 4
-        late_rows = wb_raw[LATE][:].rearrange("p t n -> p n t")
-        nc.scalar.copy(out=wb_late[:, 0:split, :], in_=late_rows[:, first : first + split, :])
-        nc.vector.tensor_copy(out=wb_late[:, split:LATE_COLS, :], in_=late_rows[:, first + split :, :])
+        late_rows = wb_raw[LATE]
+        interleave(nc.scalar.copy, wb_late[:, 0:split, :], late_rows[:, :, first : first + split])
+        interleave(nc.vector.tensor_copy, wb_late[:, split:LATE_COLS, :], late_rows[:, :, first + split :])
         quantise_wb(LATE[0], LATE[1], slice(first, H), wb_late[:, 0:LATE_COLS, :])
-        second_layer_passes(1, range(OUT_TILES - 1, OUT_TILES))
+        second_layer_passes(1, late_pieces)
 
-        for n in range(OUT_TILES):
-            cols = slice(n * BANK_COLS, (n + 1) * BANK_COLS)
-            if n == 2:
-                nc.vector.tensor_copy(out=out_sb[:, cols], in_=out_ps[n][:])
-            else:
-                nc.scalar.copy(out=out_sb[:, cols], in_=out_ps[n][:])
-            nc.sync.dma_start(out=out_rows[:, cols], in_=out_sb[:, cols])
+        scalar, vector = nc.scalar.copy, nc.vector.tensor_copy
+        for n, copy in enumerate((scalar, scalar, vector, scalar, scalar, vector)):
+            copy(out=out_sb[:, pieces[n]], in_=out_ps[n][:])
+            if n not in late_pieces:
+                nc.sync.dma_start(out=out_rows[:, pieces[n]], in_=out_sb[:, pieces[n]])
+        late_cols = slice(OUT_COLS - LATE_COLS, OUT_COLS)
+        nc.sync.dma_start(out=out_rows[:, late_cols], in_=out_sb[:, late_cols])

from contextlib import ExitStack

import concourse.mybir as mybir
from concourse.masks import make_identity

F32 = mybir.dt.float32
BF16 = mybir.dt.bfloat16
I32 = mybir.dt.int32
U32 = mybir.dt.uint32
U8 = mybir.dt.uint8
FP8X4 = mybir.dt.float8_e4m3fn_x4
RELU = mybir.ActivationFunctionType.Relu
COPY = mybir.ActivationFunctionType.Copy
ADD = mybir.AluOpType.add
MAX = mybir.AluOpType.max

P = 128
PACK = 4
ALIGN = 256
K_PASS = P * PACK
SEQS = 2
SEQ_LEN = 64
TOKENS = SEQS * SEQ_LEN
NIN = 8192
CTX = 3
H = 1024
NOUT = 2
OUT_COLS = NOUT * H

X_GROUPS = NIN // K_PASS
W_GROUPS = CTX * X_GROUPS
H_TILES = H // P
H_PASSES = H // K_PASS
BANK_COLS = 512
PSUM_BANKS = 8
OUT_TILES = OUT_COLS // BANK_COLS

X_QUARTER = 4
GROUPS_PER_BANK = 2
W_CHUNK = 2
W_CHUNKS = W_GROUPS // W_CHUNK
LAST_PAIR = W_CHUNKS - 2
W_BUFS = 6
SCALE_ROWS = K_PASS // 32
PLANE_STEP = 4
SCALE_BATCH = 2 * CTX
SCALE_BATCHES = CTX * SCALE_ROWS // SCALE_BATCH

LATE = (NOUT - 1, H_PASSES - 1)
LATE_COLS = BANK_COLS

HERE, BEFORE, AFTER = 0, 1, 2

FLOPS = 2 * TOKENS * (CTX * NIN * H + H * OUT_COLS)


def tile_bilinearpairedlayer_pa_k_kernel(tc, x_l, W_l_words, W_l_scales, b_l, W_bil, out):
    nc = tc.nc
    x_rows = x_l.flatten_outer_dims()
    out_rows = out.rearrange("b i k g -> (b i) (k g)")
    w_rows = W_l_words.rearrange("g p n t -> p g (n t)").bitcast(I32)
    scale_rows = W_l_scales.rearrange("(c g) q n -> c q g n", c=CTX).bitcast(I32)

    with ExitStack() as stack:
        keep = stack.enter_context(tc.tile_pool(name="keep", bufs=1))
        w_ring = stack.enter_context(tc.tile_pool(name="w_ring", bufs=W_BUFS))
        wb_raw_pool = stack.enter_context(tc.tile_pool(name="wb_raw", bufs=NOUT * H_PASSES))
        wb_grouped_pool = stack.enter_context(tc.tile_pool(name="wb_grouped", bufs=1))
        psum = stack.enter_context(tc.psum_pool(name="psum", bufs=PSUM_BANKS))
        stack.enter_context(tc.manual_schedule())

        ident = keep.tile([P, P], F32)
        zeros = keep.tile([P, X_GROUPS, SEQS, PACK], BF16)
        bias_rows = keep.tile([P, P], BF16)
        bias_rows_f32 = keep.tile([P, P], F32)
        bias = keep.tile([P, H_TILES], F32)
        x_raw = keep.tile([P, NIN], BF16, align_bytes=ALIGN)
        x_here = keep.tile([P, X_GROUPS, TOKENS, PACK], BF16, align_bytes=ALIGN)
        x_before = keep.tile([P, X_GROUPS, TOKENS, PACK], BF16, align_bytes=ALIGN)
        x_after = keep.tile([P, X_GROUPS, TOKENS, PACK], BF16, align_bytes=ALIGN)
        xq_words = keep.tile([P, CTX, X_GROUPS, TOKENS], U32, align_bytes=ALIGN)
        xq_planes = keep.tile([P, CTX, X_GROUPS, TOKENS], U8, align_bytes=ALIGN)
        w_planes = keep.tile([P, X_GROUPS, H], U8, align_bytes=ALIGN)
        wb_words = keep.tile([P, H_PASSES, OUT_COLS], U32, align_bytes=ALIGN)
        wb_planes = keep.tile([P, H_PASSES, OUT_COLS], U8, align_bytes=ALIGN)
        hl_t = keep.tile([P, H_TILES, TOKENS], BF16)
        hl_grouped = keep.tile([P, H_PASSES, TOKENS, PACK], BF16, align_bytes=ALIGN)
        hl_words = keep.tile([P, H_PASSES, TOKENS], U32, align_bytes=ALIGN)
        hl_planes = keep.tile([P, H_PASSES, TOKENS], U8, align_bytes=ALIGN)
        out_sb = keep.tile([P, OUT_COLS], F32, align_bytes=ALIGN)

        nc.vector.memset(bias_rows[:], 0.0)
        nc.vector.memset(w_planes[:].bitcast(I32), 0)
        nc.vector.memset(zeros[:], 0.0)
        make_identity(nc, ident[:])

        nc.scalar.dma_start(out=bias_rows[0:H_TILES, :], in_=b_l.rearrange("(j p) -> j p", p=P))

        def load_scale_batch(batch):
            odd, r = divmod(batch, 4)
            for upper in range(2):
                quad = 2 * upper + odd
                q = 4 * quad + r
                for c in range(CTX):
                    row = 32 * quad + PLANE_STEP * c + r
                    nc.sync.dma_start(
                        out=w_planes[row : row + 1, :, :].bitcast(I32), in_=scale_rows[c, q : q + 1, :, :]
                    )

        def large_load(number, out, in_):
            nc.sync.dma_start(out=out, in_=in_)
            if number < SCALE_BATCHES:
                load_scale_batch(number)

        large_load(0, x_raw[:], x_rows)

        def wb_rows(k, s):
            return W_bil[k, s * K_PASS : (s + 1) * K_PASS, :].rearrange("(t p) n -> p t n", p=P)

        wb_raw = {}
        for k in range(NOUT):
            for s in range(H_PASSES):
                raw = wb_raw_pool.tile([P, PACK, H], BF16, name="wb_raw", align_bytes=ALIGN)
                wb_raw[(k, s)] = raw
                if (k, s) != LATE:
                    large_load(1 + k * H_PASSES + s, raw[:], wb_rows(k, s))

        def load_part(i, s, g0, g1):
            units = slice(s * K_PASS, (s + 1) * K_PASS)
            groups = slice(i * W_CHUNK + g0, i * W_CHUNK + g1)
            nc.sync.dma_start(out=w_chunks[i][:, g0:g1, units].bitcast(I32), in_=w_rows[:, groups, units])

        def load_w_chunk(i):
            w_chunks[i] = w_ring.tile([P, W_CHUNK, H], U32, align_bytes=ALIGN, name="w")
            if i < LAST_PAIR:
                groups = slice(i * W_CHUNK, (i + 1) * W_CHUNK)
                large_load(NOUT * H_PASSES + i, w_chunks[i][:].bitcast(I32), w_rows[:, groups, :])
            else:
                load_part(i, 0, 0, W_CHUNK)
            if i == W_CHUNKS - 1:
                load_part(LAST_PAIR, 1, 0, W_CHUNK)
                for g in range(W_CHUNK):
                    load_part(i, 1, g, g + 1)
                late = slice(H - LATE_COLS, H)
                nc.sync.dma_start(out=wb_raw[LATE][:, :, late], in_=wb_rows(*LATE)[:, :, late])

        w_chunks = {}
        for i in range(W_BUFS):
            load_w_chunk(i)
            if i == 3:
                nc.sync.dma_start(out=wb_raw[LATE][:, :, 0 : H - LATE_COLS], in_=wb_rows(*LATE)[:, :, 0 : H - LATE_COLS])

        def interleave(copy, grouped, rows):
            copy(
                out=grouped.rearrange("p (c i) t -> p c t i", i=4),
                in_=rows.rearrange("p t (c i) -> p c t i", i=4),
            )

        def quantise_x(x_tile, c, quarter):
            groups = slice(quarter * X_QUARTER, (quarter + 1) * X_QUARTER)
            nc.vector.quantize_mx(
                out=xq_words[:, c, groups, :].rearrange("p g w -> p (g w)").bitcast(FP8X4),
                scales=xq_planes[:, c, groups, :].rearrange("p g w -> p (g w)"),
                in_=x_tile[:, groups, :, :].rearrange("p g w t -> p (g w t)"),
            )

        x_pairs = x_raw[:].bitcast(F32)
        pairs_per_group = K_PASS // 2
        for quarter in range(X_GROUPS // X_QUARTER):
            for half in range(X_QUARTER // GROUPS_PER_BANK):
                g0 = quarter * X_QUARTER + half * GROUPS_PER_BANK
                xt = psum.tile([P, GROUPS_PER_BANK, 2, TOKENS], F32, tag="bank")
                for g in range(GROUPS_PER_BANK):
                    for u in range(2):
                        first = (g0 + g) * pairs_per_group
                        nc.tensor.transpose(
                            xt[:, g, u, :], x_pairs[:, first + u : first + pairs_per_group : 2], ident[:]
                        )
                grouped = x_here[:, g0 : g0 + GROUPS_PER_BANK, :, :].bitcast(F32)
                if half == 0:
                    nc.scalar.copy(out=grouped, in_=xt[:].rearrange("p g u w -> p g w u"))
                else:
                    nc.vector.tensor_copy(out=grouped, in_=xt[:].rearrange("p g u w -> p g w u"))
            quantise_x(x_here, HERE, quarter)

        nc.vector.tensor_copy(out=bias_rows_f32[:], in_=bias_rows[:])
        bias_ps = psum.tile([P, P], F32, tag="bank")
        nc.tensor.transpose(bias_ps[:], bias_rows_f32[:], ident[:])
        nc.scalar.activation(out=bias[:], in_=bias_ps[:, 0:H_TILES], func=COPY)

        by_seq = "p g (b i) t -> p g b (i t)"
        here_seq = x_here[:].rearrange(by_seq, b=SEQS)
        before_seq = x_before[:].rearrange(by_seq, b=SEQS)
        after_seq = x_after[:].rearrange(by_seq, b=SEQS)
        kept = (SEQ_LEN - 1) * PACK
        nc.scalar.copy(out=before_seq[:, :, :, 0:PACK], in_=zeros[:])
        nc.scalar.copy(out=after_seq[:, :, :, kept:], in_=zeros[:])
        for quarter in range(X_GROUPS // X_QUARTER):
            groups = slice(quarter * X_QUARTER, (quarter + 1) * X_QUARTER)
            nc.scalar.copy(out=before_seq[:, groups, :, PACK:], in_=here_seq[:, groups, :, 0:kept])
            quantise_x(x_before, BEFORE, quarter)
        for quarter in range(X_GROUPS // X_QUARTER):
            groups = slice(quarter * X_QUARTER, (quarter + 1) * X_QUARTER)
            nc.scalar.copy(out=after_seq[:, groups, :, 0:kept], in_=here_seq[:, groups, :, PACK:])
            quantise_x(x_after, AFTER, quarter)

        def quantise_wb(k, s, cols, grouped):
            out_cols = slice(k * H + cols.start, k * H + cols.stop)
            nc.vector.quantize_mx(
                out=wb_words[:, s, out_cols].bitcast(FP8X4),
                scales=wb_planes[:, s, out_cols],
                in_=grouped.rearrange("p n t -> p (n t)"),
            )

        for k in range(NOUT):
            for s in range(H_PASSES):
                cols = slice(0, H - LATE_COLS if (k, s) == LATE else H)
                wb_grouped = wb_grouped_pool.tile([P, H, PACK], BF16, align_bytes=ALIGN)
                interleave(nc.vector.tensor_copy, wb_grouped[:, cols, :], wb_raw[(k, s)][:, :, cols])
                quantise_wb(k, s, cols, wb_grouped[:, cols, :])

        pre_t = [psum.tile([P, TOKENS], F32, tag="bank", name="pre_t%d" % j) for j in range(H_TILES)]
        def first_layer_passes(i, s):
            for local in range(W_CHUNK):
                group = i * W_CHUNK + local
                c, g = divmod(group, X_GROUPS)
                for j in range(s * PACK, (s + 1) * PACK):
                    units = slice(j * P, (j + 1) * P)
                    nc.tensor.matmul_mx(
                        out=pre_t[j][:],
                        lhsT=w_chunks[i][:, local, units].bitcast(FP8X4),
                        lhsT_scale=w_planes[PLANE_STEP * c : P, g, units],
                        rhs=xq_words[:, c, g, :].bitcast(FP8X4),
                        rhs_scale=xq_planes[:, c, g, :],
                        start=(group == 0),
                        stop=(group == W_GROUPS - 1),
                    )

        for i in range(LAST_PAIR):
            for s in range(H_PASSES):
                first_layer_passes(i, s)
            if i + W_BUFS < W_CHUNKS:
                load_w_chunk(i + W_BUFS)
        for s in range(H_PASSES):
            for i in range(LAST_PAIR, W_CHUNKS):
                first_layer_passes(i, s)

        def hidden_to_words(s):
            for t in range(PACK):
                j = s * PACK + t
                if t % 2 == 0:
                    nc.scalar.activation(
                        out=hl_t[:, j, :], in_=pre_t[j][:], func=RELU, bias=bias[:, j : j + 1], scale=1.0
                    )
                else:
                    nc.vector.tensor_scalar(
                        out=hl_t[:, j, :], in0=pre_t[j][:], scalar1=bias[:, j : j + 1], scalar2=0.0, op0=ADD, op1=MAX
                    )
            tiles = slice(s * PACK, (s + 1) * PACK)
            interleave(nc.vector.tensor_copy, hl_grouped[:, s, :, :], hl_t[:, tiles, :])
            nc.vector.quantize_mx(
                out=hl_words[:, s, :].bitcast(FP8X4),
                scales=hl_planes[:, s, :],
                in_=hl_grouped[:, s, :, :].rearrange("p w t -> p (w t)"),
            )

        cuts = [0, 256, 768, 1280, 1536, 1792, 2048]
        pieces = [slice(lo, hi) for lo, hi in zip(cuts[:-1], cuts[1:])]
        late_pieces = (4, 5)

        def second_layer_passes(s, numbers):
            for n in numbers:
                if s == 0:
                    out_ps[n] = psum.tile([P, pieces[n].stop - pieces[n].start], F32, tag="bank", name="out_ps%d" % n)
                nc.tensor.matmul_mx(
                    out=out_ps[n][:],
                    lhsT=hl_words[:, s, :].bitcast(FP8X4),
                    lhsT_scale=hl_planes[:, s, :],
                    rhs=wb_words[:, s, pieces[n]].bitcast(FP8X4),
                    rhs_scale=wb_planes[:, s, pieces[n]],
                    start=(s == 0),
                    stop=(s == H_PASSES - 1),
                )

        out_ps = {}
        hidden_to_words(0)
        second_layer_passes(0, range(4))
        hidden_to_words(1)
        second_layer_passes(1, range(4))
        second_layer_passes(0, late_pieces)

        wb_late = wb_grouped_pool.tile([P, H, PACK], BF16, align_bytes=ALIGN, name="wb_grouped")
        first = H - LATE_COLS
        split = LATE_COLS // 4
        late_rows = wb_raw[LATE]
        interleave(nc.scalar.copy, wb_late[:, 0:split, :], late_rows[:, :, first : first + split])
        interleave(nc.vector.tensor_copy, wb_late[:, split:LATE_COLS, :], late_rows[:, :, first + split :])
        quantise_wb(LATE[0], LATE[1], slice(first, H), wb_late[:, 0:LATE_COLS, :])
        second_layer_passes(1, late_pieces)

        scalar, vector = nc.scalar.copy, nc.vector.tensor_copy
        for n, copy in enumerate((scalar, scalar, vector, scalar, scalar, vector)):
            copy(out=out_sb[:, pieces[n]], in_=out_ps[n][:])
            if n not in late_pieces:
                nc.sync.dma_start(out=out_rows[:, pieces[n]], in_=out_sb[:, pieces[n]])
        late_cols = slice(OUT_COLS - LATE_COLS, OUT_COLS)
        nc.sync.dma_start(out=out_rows[:, late_cols], in_=out_sb[:, late_cols])
